import numpy as np
import ml_dtypes


def mxq(x, axis, fmt="e4m3"):
    dtype, down = {"e4m3": (ml_dtypes.float8_e4m3fn, 7), "e5m2": (ml_dtypes.float8_e5m2, 14)}[fmt]
    v = np.moveaxis(np.asarray(x, np.float32).astype(ml_dtypes.bfloat16).astype(np.float64), axis, -1)
    blocks = v.reshape(v.shape[:-1] + (-1, 32))
    amax = np.abs(blocks).max(-1, keepdims=True)
    byte = np.maximum(np.where(amax > 0, np.frexp(amax)[1] - 1 + 127, 0) - down, 1)
    scale = np.exp2(byte - 127.0)
    codes = (blocks / scale).astype(np.float32).astype(dtype).astype(np.float64)
    return np.moveaxis((codes * scale).reshape(v.shape), -1, axis)


WIDE = False


def mx_kscale(k):
    if not WIDE:
        return np.ones(k)
    levels = np.array([10, -10, 5, -5, 0])
    a = np.random.permutation(np.resize(levels, k // 512 * 4)).reshape(k // 512, 4)
    idx = np.arange(k)
    return np.exp2(a[idx // 512, idx % 128 // 32])


BF16 = ml_dtypes.bfloat16


def bf(x):
    return np.asarray(x, np.float32).astype(BF16)


def f64(x):
    return np.asarray(x).astype(np.float64)


B, C, HH, WW = 1, 512, 32, 32
N = HH * WW


def setup_inputs():
    s, t = mx_kscale(C), mx_kscale(C)
    return {"x": bf(np.random.standard_normal((B, C, HH, WW)) * s[None, :, None, None]),
            "Wq": bf(np.random.standard_normal((C, C)) * 1.4 / np.sqrt(C) * t[:, None] / s[None, :]),
            "bq": bf(np.random.standard_normal(C) * 0.2 * t),
            "k": bf(np.random.standard_normal((B, N, C)) * 1.4 / t)}


def reference(x, Wq, bq, k):
    xt = f64(x).reshape(B, C, N)
    q = (mxq(xt, 1, "e4m3").transpose(0, 2, 1) @ mxq(f64(Wq), 1, "e4m3").T) + f64(bq)
    scores = mxq(q / np.sqrt(C), 2, "e4m3") @ mxq(f64(k), 2, "e4m3").transpose(0, 2, 1)
    e = np.exp(scores - scores.max(-1, keepdims=True))
    return e / e.sum(-1, keepdims=True)

@@ -1,0 +1,187 @@
+import math
+from contextlib import ExitStack
+
+import concourse.masks as masks
+import concourse.mybir as mybir
+
+F32 = mybir.dt.float32
+BF16 = mybir.dt.bfloat16
+U32 = mybir.dt.uint32
+U8 = mybir.dt.uint8
+FP8X4 = mybir.dt.float8_e4m3fn_x4
+ACT = mybir.ActivationFunctionType
+ALU = mybir.AluOpType
+AXIS = mybir.AxisListType
+
+P = 128
+PACK = 4
+CHANNELS = P * PACK
+TOKENS = 1024
+HALF = 512
+HALVES = TOKENS // HALF
+WORD_PAIR = 2
+INV_SQRT_CHANNELS = 1.0 / math.sqrt(CHANNELS)
+
+FLOPS = 2 * TOKENS * CHANNELS * CHANNELS + 2 * TOKENS * TOKENS * CHANNELS
+
+
+def quantise(nc, pool, grouped, label):
+    codes = pool.tile([P, HALF], U32, name="%s_codes" % label, align_bytes=64)
+    scales = pool.tile([P, HALF], U8, name="%s_scales" % label, align_bytes=64)
+    nc.vector.quantize_mx(out=codes[:].bitcast(FP8X4), scales=scales[:], in_=grouped[:])
+    return codes, scales
+
+
+def interleave_planes(nc, pool, planes, label):
+    grouped = pool.tile([P, HALF * PACK], BF16, name="%s_grouped" % label, align_bytes=64)
+    nc.vector.tensor_copy(
+        out=grouped[:].rearrange("p (c i t) -> p c t i", i=4, t=PACK),
+        in_=planes[:].rearrange("p t (c i) -> p c t i", i=4),
+    )
+    return grouped
+
+
+def channels_to_partitions(nc, pool, psum, identity, rows, label):
+    row_words = rows[:].bitcast(F32).rearrange("p (a w u) -> p a u w", a=PACK, u=WORD_PAIR)
+    grouped = pool.tile([P, HALF * PACK], BF16, name="%s_grouped" % label, align_bytes=64)
+    grouped_words = grouped[:].bitcast(F32).rearrange("p (a r u) -> p a r u", a=PACK, u=WORD_PAIR)
+    tiles_per_bank = 2
+    for first in range(0, PACK, tiles_per_bank):
+        bank = psum.tile([P, HALF], F32, tag="bank")
+        flipped = bank[:].rearrange("p (a u r) -> p a u r", a=tiles_per_bank, u=WORD_PAIR)
+        for a in range(tiles_per_bank):
+            for u in range(WORD_PAIR):
+                nc.tensor.transpose(flipped[:, a, u, :], row_words[:, first + a, u, :], identity[:])
+        nc.scalar.copy(
+            out=grouped_words[:, first : first + tiles_per_bank],
+            in_=flipped.rearrange("p a u r -> p a r u"),
+        )
+    return grouped
+
+
+def tile_visionattention_pa_kernel(tc, x, Wq, bq, k, out):
+    nc = tc.nc
+    x_planes_dram = x.rearrange("b c h w -> (b c) (h w)").rearrange("(p j) n -> p j n", j=PACK)
+    k_rows_dram = k.flatten_outer_dims()
+    out_rows_dram = out.flatten_outer_dims()
+
+    with ExitStack() as ctx:
+        keep = ctx.enter_context(tc.tile_pool(name="keep", bufs=1))
+        rows_pool = ctx.enter_context(tc.tile_pool(name="rows", bufs=4))
+        psum = ctx.enter_context(tc.psum_pool(name="psum", bufs=8))
+
+        wq_rows = keep.tile([P, PACK * CHANNELS], BF16)
+        nc.sync.dma_start(out=wq_rows[:], in_=Wq.rearrange("(r t) c -> r (t c)", t=PACK))
+        x_planes = []
+        k_rows = []
+        for h in range(HALVES):
+            cols = slice(h * HALF, (h + 1) * HALF)
+            x_half = keep.tile([P, PACK, HALF], BF16, name="x_planes%d" % h)
+            nc.sync.dma_start(out=x_half[:], in_=x_planes_dram[:, :, cols])
+            x_planes.append(x_half)
+            k_half = keep.tile([P, PACK * CHANNELS], BF16, name="k_rows%d" % h)
+            nc.sync.dma_start(
+                out=k_half[:].rearrange("r (a c) -> r a c", a=PACK),
+                in_=k_rows_dram[cols, :].rearrange("(a r) c -> r a c", r=P),
+            )
+            k_rows.append(k_half)
+        bq_raw = keep.tile([P, PACK], BF16)
+        nc.scalar.dma_start(out=bq_raw[:], in_=bq.rearrange("(r t) -> r t", t=PACK))
+
+        identity = keep.tile([P, P], F32)
+        masks.make_identity(nc, identity[:])
+        warm = keep.tile([P, 1], F32)
+        nc.vector.memset(warm[:], 0.0)
+        nc.scalar.activation(out=warm[:], in_=warm[:], func=ACT.Exp)
+        bias = keep.tile([P, PACK], F32)
+        nc.vector.tensor_scalar_mul(out=bias[:], in0=bq_raw[:], scalar1=INV_SQRT_CHANNELS)
+
+        wq_grouped = channels_to_partitions(nc, keep, psum, identity, wq_rows, "wq")
+        wq_codes, wq_scales = quantise(nc, keep, wq_grouped, "wq")
+
+        x_mx = []
+        k_mx = []
+        for h in range(HALVES):
+            x_grouped = interleave_planes(nc, keep, x_planes[h], "x%d" % h)
+            x_mx.append(quantise(nc, keep, x_grouped, "x%d" % h))
+            k_grouped = channels_to_partitions(nc, keep, psum, identity, k_rows[h], "k%d" % h)
+            k_mx.append(quantise(nc, keep, k_grouped, "k%d" % h))
+
+        q_mx = []
+        for h in range(HALVES):
+            x_codes, x_scales = x_mx[h]
+            q_planes = keep.tile([P, PACK, HALF], BF16, name="q_planes%d" % h)
+            for t in range(PACK):
+                out_channels = slice(t * P, (t + 1) * P)
+                bank = psum.tile([P, HALF], F32, tag="bank")
+                nc.tensor.matmul_mx(
+                    out=bank[:],
+                    lhsT=wq_codes[:, out_channels].bitcast(FP8X4),
+                    lhsT_scale=wq_scales[:, out_channels],
+                    rhs=x_codes[:].bitcast(FP8X4),
+                    rhs_scale=x_scales[:],
+                    start=True,
+                    stop=True,
+                )
+                nc.scalar.activation(
+                    out=q_planes[:, t, :],
+                    in_=bank[:],
+                    func=ACT.Identity,
+                    bias=bias[:, t : t + 1],
+                    scale=INV_SQRT_CHANNELS,
+                )
+            q_grouped = interleave_planes(nc, keep, q_planes, "q%d" % h)
+            q_mx.append(quantise(nc, keep, q_grouped, "q%d" % h))
+
+        for i in range(TOKENS // P):
+            q_codes, q_scales = q_mx[(i * P) // HALF]
+            tokens = slice((i * P) % HALF, (i * P) % HALF + P)
+            score_banks = []
+            maxes = rows_pool.tile([P, HALVES], F32)
+            for h in range(HALVES):
+                k_codes, k_scales = k_mx[h]
+                bank = psum.tile([P, HALF], F32, tag="bank")
+                nc.tensor.matmul_mx(
+                    out=bank[:],
+                    lhsT=q_codes[:, tokens].bitcast(FP8X4),
+                    lhsT_scale=q_scales[:, tokens],
+                    rhs=k_codes[:].bitcast(FP8X4),
+                    rhs_scale=k_scales[:],
+                    start=True,
+                    stop=True,
+                )
+                nc.vector.tensor_reduce(out=maxes[:, h : h + 1], in_=bank[:], axis=AXIS.X, op=ALU.max)
+                score_banks.append(bank)
+            neg_max = rows_pool.tile([P, 1], F32)
+            nc.vector.tensor_scalar(
+                out=neg_max[:],
+                in0=maxes[:, 0:1],
+                scalar1=maxes[:, 1:2],
+                scalar2=-1.0,
+                op0=ALU.max,
+                op1=ALU.mult,
+            )
+            probs = rows_pool.tile([P, TOKENS], F32)
+            sums = rows_pool.tile([P, HALVES], F32)
+            for h in range(HALVES):
+                nc.scalar.activation(
+                    out=probs[:, h * HALF : (h + 1) * HALF],
+                    in_=score_banks[h][:],
+                    func=ACT.Exp,
+                    bias=neg_max[:, 0:1],
+                    scale=1.0,
+                    accum_out=sums[:, h : h + 1],
+                )
+            row_sum = rows_pool.tile([P, 1], F32)
+            nc.vector.tensor_add(out=row_sum[:], in0=sums[:, 0:1], in1=sums[:, 1:2])
+            inv_sum = rows_pool.tile([P, 1], F32)
+            nc.vector.reciprocal(out=inv_sum[:], in_=row_sum[:])
+            nc.gpsimd.tensor_scalar(
+                out=probs[:],
+                in0=probs[:],
+                scalar1=inv_sum[:, 0:1],
+                scalar2=0.0,
+                op0=ALU.mult,
+                op1=ALU.add,
+            )
+            nc.sync.dma_start(out=out_rows_dram[i * P : (i + 1) * P, :], in_=probs[:])

@@ -19,15 +19,21 @@ CHANNELS = P * PACK
 TOKENS = 1024
 HALF = 512
 HALVES = TOKENS // HALF
+TILES = TOKENS // P
+TILES_PER_HALF = HALF // P
 WORD_PAIR = 2
 INV_SQRT_CHANNELS = 1.0 / math.sqrt(CHANNELS)
+LEAD = 4
+PACK_LEAD = LEAD - 2
+LAG = 2
 
 FLOPS = 2 * TOKENS * CHANNELS * CHANNELS + 2 * TOKENS * TOKENS * CHANNELS
 
 
 def quantise(nc, pool, grouped, label):
-    codes = pool.tile([P, HALF], U32, name="%s_codes" % label, align_bytes=64)
-    scales = pool.tile([P, HALF], U8, name="%s_scales" % label, align_bytes=64)
+    width = grouped.shape[1] // PACK
+    codes = pool.tile([P, width], U32, name="%s_codes" % label, tag="%s_codes" % label, align_bytes=64)
+    scales = pool.tile([P, width], U8, name="%s_scales" % label, tag="%s_scales" % label, align_bytes=64)
     nc.vector.quantize_mx(out=codes[:].bitcast(FP8X4), scales=scales[:], in_=grouped[:])
     return codes, scales
 
@@ -66,23 +72,26 @@ def tile_visionattention_pa_kernel(tc, x, Wq, bq, k, out):
     out_rows_dram = out.flatten_outer_dims()
 
     with ExitStack() as ctx:
+        ctx.enter_context(tc.manual_schedule())
         keep = ctx.enter_context(tc.tile_pool(name="keep", bufs=1))
-        rows_pool = ctx.enter_context(tc.tile_pool(name="rows", bufs=4))
-        psum = ctx.enter_context(tc.psum_pool(name="psum", bufs=8))
+        q_pool = ctx.enter_context(tc.tile_pool(name="q", bufs=LEAD + 1))
+        row_pool = ctx.enter_context(tc.tile_pool(name="rows", bufs=LAG + 3))
+        banks = ctx.enter_context(tc.psum_pool(name="banks", bufs=6))
+        q_banks = ctx.enter_context(tc.psum_pool(name="q_banks", bufs=2))
 
         wq_rows = keep.tile([P, PACK * CHANNELS], BF16)
         nc.sync.dma_start(out=wq_rows[:], in_=Wq.rearrange("(r t) c -> r (t c)", t=PACK))
         x_planes = []
+        for h in range(HALVES):
+            x_half = keep.tile([P, PACK, HALF], BF16, name="x_planes%d" % h)
+            nc.sync.dma_start(out=x_half[:], in_=x_planes_dram[:, :, h * HALF : (h + 1) * HALF])
+            x_planes.append(x_half)
         k_rows = []
         for h in range(HALVES):
-            cols = slice(h * HALF, (h + 1) * HALF)
-            x_half = keep.tile([P, PACK, HALF], BF16, name="x_planes%d" % h)
-            nc.sync.dma_start(out=x_half[:], in_=x_planes_dram[:, :, cols])
-            x_planes.append(x_half)
             k_half = keep.tile([P, PACK * CHANNELS], BF16, name="k_rows%d" % h)
             nc.sync.dma_start(
                 out=k_half[:].rearrange("r (a c) -> r a c", a=PACK),
-                in_=k_rows_dram[cols, :].rearrange("(a r) c -> r a c", r=P),
+                in_=k_rows_dram[h * HALF : (h + 1) * HALF, :].rearrange("(a r) c -> r a c", r=P),
             )
             k_rows.append(k_half)
         bq_raw = keep.tile([P, PACK], BF16)
@@ -93,95 +102,166 @@ def tile_visionattention_pa_kernel(tc, x, Wq, bq, k, out):
         warm = keep.tile([P, 1], F32)
         nc.vector.memset(warm[:], 0.0)
         nc.scalar.activation(out=warm[:], in_=warm[:], func=ACT.Exp)
+
+        wq_grouped = channels_to_partitions(nc, keep, banks, identity, wq_rows, "wq")
+        x_grouped = [interleave_planes(nc, keep, x_planes[h], "x%d" % h) for h in range(HALVES)]
+        wq_codes, wq_scales = quantise(nc, keep, wq_grouped, "wq")
+        x_mx = [quantise(nc, keep, x_grouped[h], "x%d" % h) for h in range(HALVES)]
         bias = keep.tile([P, PACK], F32)
         nc.vector.tensor_scalar_mul(out=bias[:], in0=bq_raw[:], scalar1=INV_SQRT_CHANNELS)
 
-        wq_grouped = channels_to_partitions(nc, keep, psum, identity, wq_rows, "wq")
-        wq_codes, wq_scales = quantise(nc, keep, wq_grouped, "wq")
-
-        x_mx = []
+        q_psum = {}
+        q_grouped = {}
+        q_mx = {}
         k_mx = []
-        for h in range(HALVES):
-            x_grouped = interleave_planes(nc, keep, x_planes[h], "x%d" % h)
-            x_mx.append(quantise(nc, keep, x_grouped, "x%d" % h))
-            k_grouped = channels_to_partitions(nc, keep, psum, identity, k_rows[h], "k%d" % h)
-            k_mx.append(quantise(nc, keep, k_grouped, "k%d" % h))
+        scores = {}
+        maxes = {}
+        neg_max = {}
+        probs = {}
+        sums = {}
+        row_sum = {}
+        inv_sum = {}
 
-        q_mx = []
-        for h in range(HALVES):
-            x_codes, x_scales = x_mx[h]
-            q_planes = keep.tile([P, PACK, HALF], BF16, name="q_planes%d" % h)
+        def project(g):
+            x_codes, x_scales = x_mx[g // TILES_PER_HALF]
+            tokens = slice((g % TILES_PER_HALF) * P, (g % TILES_PER_HALF + 1) * P)
+            products = q_banks.tile([P, PACK, P], F32, tag="products")
             for t in range(PACK):
                 out_channels = slice(t * P, (t + 1) * P)
-                bank = psum.tile([P, HALF], F32, tag="bank")
                 nc.tensor.matmul_mx(
-                    out=bank[:],
+                    out=products[:, t, :],
                     lhsT=wq_codes[:, out_channels].bitcast(FP8X4),
                     lhsT_scale=wq_scales[:, out_channels],
-                    rhs=x_codes[:].bitcast(FP8X4),
-                    rhs_scale=x_scales[:],
+                    rhs=x_codes[:, tokens].bitcast(FP8X4),
+                    rhs_scale=x_scales[:, tokens],
                     start=True,
                     stop=True,
                 )
-                nc.scalar.activation(
-                    out=q_planes[:, t, :],
-                    in_=bank[:],
-                    func=ACT.Identity,
-                    bias=bias[:, t : t + 1],
-                    scale=INV_SQRT_CHANNELS,
-                )
-            q_grouped = interleave_planes(nc, keep, q_planes, "q%d" % h)
-            q_mx.append(quantise(nc, keep, q_grouped, "q%d" % h))
+            q_psum[g] = products
 
-        for i in range(TOKENS // P):
-            q_codes, q_scales = q_mx[(i * P) // HALF]
-            tokens = slice((i * P) % HALF, (i * P) % HALF + P)
-            score_banks = []
-            maxes = rows_pool.tile([P, HALVES], F32)
+        def leave_psum(g):
+            grouped = q_pool.tile([P, P * PACK], BF16, tag="q_grouped", align_bytes=64)
+            nc.vector.scalar_tensor_tensor(
+                out=grouped[:].rearrange("p (n t) -> p n t", t=PACK),
+                in0=q_psum[g][:].rearrange("p t n -> p n t"),
+                scalar=INV_SQRT_CHANNELS,
+                in1=bias[:].unsqueeze(1).to_broadcast([P, P, PACK]),
+                op0=ALU.mult,
+                op1=ALU.add,
+            )
+            q_grouped[g] = grouped
+
+        def pack(g):
+            q_mx[g] = quantise(nc, q_pool, q_grouped[g], "q")
+
+        def score(g):
+            q_codes, q_scales = q_mx[g]
+            scores[g] = []
             for h in range(HALVES):
                 k_codes, k_scales = k_mx[h]
-                bank = psum.tile([P, HALF], F32, tag="bank")
+                bank = banks.tile([P, HALF], F32, tag="bank")
                 nc.tensor.matmul_mx(
                     out=bank[:],
-                    lhsT=q_codes[:, tokens].bitcast(FP8X4),
-                    lhsT_scale=q_scales[:, tokens],
+                    lhsT=q_codes[:].bitcast(FP8X4),
+                    lhsT_scale=q_scales[:],
                     rhs=k_codes[:].bitcast(FP8X4),
                     rhs_scale=k_scales[:],
                     start=True,
                     stop=True,
                 )
-                nc.vector.tensor_reduce(out=maxes[:, h : h + 1], in_=bank[:], axis=AXIS.X, op=ALU.max)
-                score_banks.append(bank)
-            neg_max = rows_pool.tile([P, 1], F32)
+                scores[g].append(bank)
+
+        def bank_maximum(g, h):
+            if h == 0:
+                bank_maxes = row_pool.tile([P, HALVES], F32, tag="maxes")
+                maxes[g] = bank_maxes
+            nc.vector.tensor_reduce(
+                out=maxes[g][:, h : h + 1], in_=scores[g][h][:], axis=AXIS.X, op=ALU.max
+            )
+
+        def negate_maximum(g):
+            minus = row_pool.tile([P, 1], F32, tag="neg_max")
             nc.vector.tensor_scalar(
-                out=neg_max[:],
-                in0=maxes[:, 0:1],
-                scalar1=maxes[:, 1:2],
+                out=minus[:],
+                in0=maxes[g][:, 0:1],
+                scalar1=maxes[g][:, 1:2],
                 scalar2=-1.0,
                 op0=ALU.max,
                 op1=ALU.mult,
             )
-            probs = rows_pool.tile([P, TOKENS], F32)
-            sums = rows_pool.tile([P, HALVES], F32)
+            neg_max[g] = minus
+
+        def exponentials(g):
+            row_tile = row_pool.tile([P, TOKENS], F32, tag="probs")
+            bank_sums = row_pool.tile([P, HALVES], F32, tag="sums")
             for h in range(HALVES):
                 nc.scalar.activation(
-                    out=probs[:, h * HALF : (h + 1) * HALF],
-                    in_=score_banks[h][:],
+                    out=row_tile[:, h * HALF : (h + 1) * HALF],
+                    in_=scores[g][h][:],
                     func=ACT.Exp,
-                    bias=neg_max[:, 0:1],
+                    bias=neg_max[g][:, 0:1],
                     scale=1.0,
-                    accum_out=sums[:, h : h + 1],
+                    accum_out=bank_sums[:, h : h + 1],
                 )
-            row_sum = rows_pool.tile([P, 1], F32)
-            nc.vector.tensor_add(out=row_sum[:], in0=sums[:, 0:1], in1=sums[:, 1:2])
-            inv_sum = rows_pool.tile([P, 1], F32)
-            nc.vector.reciprocal(out=inv_sum[:], in_=row_sum[:])
+            probs[g] = row_tile
+            sums[g] = bank_sums
+
+        def add_sums(g):
+            total = row_pool.tile([P, 1], F32, tag="row_sum")
+            nc.vector.tensor_add(out=total[:], in0=sums[g][:, 0:1], in1=sums[g][:, 1:2])
+            row_sum[g] = total
+
+        def invert_sum(g):
+            inverse = row_pool.tile([P, 1], F32, tag="inv_sum")
+            nc.vector.reciprocal(out=inverse[:], in_=row_sum[g][:])
+            inv_sum[g] = inverse
+
+        def scale_and_store(g):
             nc.gpsimd.tensor_scalar(
-                out=probs[:],
-                in0=probs[:],
-                scalar1=inv_sum[:, 0:1],
+                out=probs[g][:],
+                in0=probs[g][:],
+                scalar1=inv_sum[g][:, 0:1],
                 scalar2=0.0,
                 op0=ALU.mult,
                 op1=ALU.add,
             )
-            nc.sync.dma_start(out=out_rows_dram[i * P : (i + 1) * P, :], in_=probs[:])
+            nc.sync.dma_start(out=out_rows_dram[g * P : (g + 1) * P, :], in_=probs[g][:])
+
+        def is_tile(g):
+            return 0 <= g < TILES
+
+        def step(s):
+            if is_tile(s + LEAD):
+                project(s + LEAD)
+            if s >= 0 and is_tile(s + 1):
+                score(s + 1)
+            if is_tile(s + LEAD):
+                leave_psum(s + LEAD)
+            if is_tile(s):
+                bank_maximum(s, 0)
+            if is_tile(s - LAG):
+                add_sums(s - LAG)
+            if is_tile(s):
+                bank_maximum(s, 1)
+            if is_tile(s + PACK_LEAD):
+                pack(s + PACK_LEAD)
+            if is_tile(s - LAG):
+                invert_sum(s - LAG)
+            if is_tile(s):
+                negate_maximum(s)
+                exponentials(s)
+            if is_tile(s - LAG):
+                scale_and_store(s - LAG)
+
+        k_grouped = []
+        k_grouped.append(channels_to_partitions(nc, keep, banks, identity, k_rows[0], "k0"))
+        step(-LEAD)
+        step(-LEAD + 1)
+        k_grouped.append(channels_to_partitions(nc, keep, banks, identity, k_rows[1], "k1"))
+        for s in range(-LEAD + 2, 0):
+            step(s)
+        for h in range(HALVES):
+            k_mx.append(quantise(nc, keep, k_grouped[h], "k%d" % h))
+        score(0)
+        for s in range(0, TILES + LAG):
+            step(s)

@@ -19,21 +19,18 @@ CHANNELS = P * PACK
 TOKENS = 1024
 HALF = 512
 HALVES = TOKENS // HALF
-TILES = TOKENS // P
-TILES_PER_HALF = HALF // P
 WORD_PAIR = 2
 INV_SQRT_CHANNELS = 1.0 / math.sqrt(CHANNELS)
-LEAD = 4
-PACK_LEAD = LEAD - 2
+TILES = TOKENS // P
+SCORE_LEAD = 2
 LAG = 2
 
 FLOPS = 2 * TOKENS * CHANNELS * CHANNELS + 2 * TOKENS * TOKENS * CHANNELS
 
 
 def quantise(nc, pool, grouped, label):
-    width = grouped.shape[1] // PACK
-    codes = pool.tile([P, width], U32, name="%s_codes" % label, tag="%s_codes" % label, align_bytes=64)
-    scales = pool.tile([P, width], U8, name="%s_scales" % label, tag="%s_scales" % label, align_bytes=64)
+    codes = pool.tile([P, HALF], U32, name="%s_codes" % label, align_bytes=64)
+    scales = pool.tile([P, HALF], U8, name="%s_scales" % label, align_bytes=64)
     nc.vector.quantize_mx(out=codes[:].bitcast(FP8X4), scales=scales[:], in_=grouped[:])
     return codes, scales
 
@@ -48,7 +45,7 @@ def interleave_planes(nc, pool, planes, label):
 
 
 def channels_to_partitions(nc, pool, psum, identity, rows, label):
-    row_words = rows[:].bitcast(F32).rearrange("p (a w u) -> p a u w", a=PACK, u=WORD_PAIR)
+    row_words = rows[:].bitcast(F32).rearrange("p (a u w) -> p a u w", a=PACK, u=WORD_PAIR)
     grouped = pool.tile([P, HALF * PACK], BF16, name="%s_grouped" % label, align_bytes=64)
     grouped_words = grouped[:].bitcast(F32).rearrange("p (a r u) -> p a r u", a=PACK, u=WORD_PAIR)
     tiles_per_bank = 2
@@ -67,53 +64,85 @@ def channels_to_partitions(nc, pool, psum, identity, rows, label):
 
 def tile_visionattention_pa_kernel(tc, x, Wq, bq, k, out):
     nc = tc.nc
-    x_planes_dram = x.rearrange("b c h w -> (b c) (h w)").rearrange("(p j) n -> p j n", j=PACK)
+    x_rows_dram = x.rearrange("b c h w -> (b c) (h w)")
     k_rows_dram = k.flatten_outer_dims()
     out_rows_dram = out.flatten_outer_dims()
 
     with ExitStack() as ctx:
-        ctx.enter_context(tc.manual_schedule())
         keep = ctx.enter_context(tc.tile_pool(name="keep", bufs=1))
-        q_pool = ctx.enter_context(tc.tile_pool(name="q", bufs=LEAD + 1))
-        row_pool = ctx.enter_context(tc.tile_pool(name="rows", bufs=LAG + 3))
-        banks = ctx.enter_context(tc.psum_pool(name="banks", bufs=6))
-        q_banks = ctx.enter_context(tc.psum_pool(name="q_banks", bufs=2))
+        rows_pool = ctx.enter_context(tc.tile_pool(name="rows", bufs=LAG + 3))
+        psum = ctx.enter_context(tc.psum_pool(name="psum", bufs=8))
 
         wq_rows = keep.tile([P, PACK * CHANNELS], BF16)
-        nc.sync.dma_start(out=wq_rows[:], in_=Wq.rearrange("(r t) c -> r (t c)", t=PACK))
+        nc.sync.dma_start(
+            out=wq_rows[:].rearrange("r (u ec) -> r u ec", u=WORD_PAIR),
+            in_=Wq.rearrange("(u r e) c -> r u (e c)", u=WORD_PAIR, e=2),
+        )
         x_planes = []
-        for h in range(HALVES):
-            x_half = keep.tile([P, PACK, HALF], BF16, name="x_planes%d" % h)
-            nc.sync.dma_start(out=x_half[:], in_=x_planes_dram[:, :, h * HALF : (h + 1) * HALF])
-            x_planes.append(x_half)
         k_rows = []
         for h in range(HALVES):
+            cols = slice(h * HALF, (h + 1) * HALF)
+            x_half = keep.tile([P, PACK, HALF], BF16, name="x_planes%d" % h)
+            for u in range(WORD_PAIR):
+                nc.sync.dma_start(
+                    out=x_half[:, 2 * u : 2 * u + 2, :],
+                    in_=x_rows_dram[u * 2 * P : (u + 1) * 2 * P, cols].rearrange("(p e) n -> p e n", e=2),
+                )
+            x_planes.append(x_half)
             k_half = keep.tile([P, PACK * CHANNELS], BF16, name="k_rows%d" % h)
-            nc.sync.dma_start(
-                out=k_half[:].rearrange("r (a c) -> r a c", a=PACK),
-                in_=k_rows_dram[h * HALF : (h + 1) * HALF, :].rearrange("(a r) c -> r a c", r=P),
-            )
+            nc.sync.dma_start(out=k_half[:], in_=k_rows_dram[cols, :].rearrange("(r a) c -> r (a c)", a=PACK))
             k_rows.append(k_half)
         bq_raw = keep.tile([P, PACK], BF16)
-        nc.scalar.dma_start(out=bq_raw[:], in_=bq.rearrange("(r t) -> r t", t=PACK))
+        nc.scalar.dma_start(
+            out=bq_raw[:].rearrange("r (u e) -> r u e", u=WORD_PAIR),
+            in_=bq.rearrange("(u r e) -> r u e", u=WORD_PAIR, e=2),
+        )
 
         identity = keep.tile([P, P], F32)
         masks.make_identity(nc, identity[:])
         warm = keep.tile([P, 1], F32)
         nc.vector.memset(warm[:], 0.0)
         nc.scalar.activation(out=warm[:], in_=warm[:], func=ACT.Exp)
-
-        wq_grouped = channels_to_partitions(nc, keep, banks, identity, wq_rows, "wq")
-        x_grouped = [interleave_planes(nc, keep, x_planes[h], "x%d" % h) for h in range(HALVES)]
-        wq_codes, wq_scales = quantise(nc, keep, wq_grouped, "wq")
-        x_mx = [quantise(nc, keep, x_grouped[h], "x%d" % h) for h in range(HALVES)]
         bias = keep.tile([P, PACK], F32)
         nc.vector.tensor_scalar_mul(out=bias[:], in0=bq_raw[:], scalar1=INV_SQRT_CHANNELS)
 
-        q_psum = {}
-        q_grouped = {}
-        q_mx = {}
+        wq_grouped = channels_to_partitions(nc, keep, psum, identity, wq_rows, "wq")
+        wq_codes, wq_scales = quantise(nc, keep, wq_grouped, "wq")
+
+        x_mx = []
         k_mx = []
+        for h in range(HALVES):
+            x_grouped = interleave_planes(nc, keep, x_planes[h], "x%d" % h)
+            x_mx.append(quantise(nc, keep, x_grouped, "x%d" % h))
+            k_grouped = channels_to_partitions(nc, keep, psum, identity, k_rows[h], "k%d" % h)
+            k_mx.append(quantise(nc, keep, k_grouped, "k%d" % h))
+
+        q_mx = []
+        for h in range(HALVES):
+            x_codes, x_scales = x_mx[h]
+            q_planes = keep.tile([P, PACK, HALF], BF16, name="q_planes%d" % h)
+            for t in range(PACK):
+                out_channels = slice(t * P, (t + 1) * P)
+                bank = psum.tile([P, HALF], F32, tag="bank")
+                nc.tensor.matmul_mx(
+                    out=bank[:],
+                    lhsT=wq_codes[:, out_channels].bitcast(FP8X4),
+                    lhsT_scale=wq_scales[:, out_channels],
+                    rhs=x_codes[:].bitcast(FP8X4),
+                    rhs_scale=x_scales[:],
+                    start=True,
+                    stop=True,
+                )
+                nc.scalar.activation(
+                    out=q_planes[:, t, :],
+                    in_=bank[:],
+                    func=ACT.Identity,
+                    bias=bias[:, t : t + 1],
+                    scale=INV_SQRT_CHANNELS,
+                )
+            q_grouped = interleave_planes(nc, keep, q_planes, "q%d" % h)
+            q_mx.append(quantise(nc, keep, q_grouped, "q%d" % h))
+
         scores = {}
         maxes = {}
         neg_max = {}
@@ -122,48 +151,17 @@ def tile_visionattention_pa_kernel(tc, x, Wq, bq, k, out):
         row_sum = {}
         inv_sum = {}
 
-        def project(g):
-            x_codes, x_scales = x_mx[g // TILES_PER_HALF]
-            tokens = slice((g % TILES_PER_HALF) * P, (g % TILES_PER_HALF + 1) * P)
-            products = q_banks.tile([P, PACK, P], F32, tag="products")
-            for t in range(PACK):
-                out_channels = slice(t * P, (t + 1) * P)
-                nc.tensor.matmul_mx(
-                    out=products[:, t, :],
-                    lhsT=wq_codes[:, out_channels].bitcast(FP8X4),
-                    lhsT_scale=wq_scales[:, out_channels],
-                    rhs=x_codes[:, tokens].bitcast(FP8X4),
-                    rhs_scale=x_scales[:, tokens],
-                    start=True,
-                    stop=True,
-                )
-            q_psum[g] = products
-
-        def leave_psum(g):
-            grouped = q_pool.tile([P, P * PACK], BF16, tag="q_grouped", align_bytes=64)
-            nc.vector.scalar_tensor_tensor(
-                out=grouped[:].rearrange("p (n t) -> p n t", t=PACK),
-                in0=q_psum[g][:].rearrange("p t n -> p n t"),
-                scalar=INV_SQRT_CHANNELS,
-                in1=bias[:].unsqueeze(1).to_broadcast([P, P, PACK]),
-                op0=ALU.mult,
-                op1=ALU.add,
-            )
-            q_grouped[g] = grouped
-
-        def pack(g):
-            q_mx[g] = quantise(nc, q_pool, q_grouped[g], "q")
-
         def score(g):
-            q_codes, q_scales = q_mx[g]
+            q_codes, q_scales = q_mx[(g * P) // HALF]
+            tokens = slice((g * P) % HALF, (g * P) % HALF + P)
             scores[g] = []
             for h in range(HALVES):
                 k_codes, k_scales = k_mx[h]
-                bank = banks.tile([P, HALF], F32, tag="bank")
+                bank = psum.tile([P, HALF], F32, tag="bank")
                 nc.tensor.matmul_mx(
                     out=bank[:],
-                    lhsT=q_codes[:].bitcast(FP8X4),
-                    lhsT_scale=q_scales[:],
+                    lhsT=q_codes[:, tokens].bitcast(FP8X4),
+                    lhsT_scale=q_scales[:, tokens],
                     rhs=k_codes[:].bitcast(FP8X4),
                     rhs_scale=k_scales[:],
                     start=True,
@@ -173,14 +171,14 @@ def tile_visionattention_pa_kernel(tc, x, Wq, bq, k, out):
 
         def bank_maximum(g, h):
             if h == 0:
-                bank_maxes = row_pool.tile([P, HALVES], F32, tag="maxes")
+                bank_maxes = rows_pool.tile([P, HALVES], F32, tag="maxes")
                 maxes[g] = bank_maxes
             nc.vector.tensor_reduce(
                 out=maxes[g][:, h : h + 1], in_=scores[g][h][:], axis=AXIS.X, op=ALU.max
             )
 
         def negate_maximum(g):
-            minus = row_pool.tile([P, 1], F32, tag="neg_max")
+            minus = rows_pool.tile([P, 1], F32, tag="neg_max")
             nc.vector.tensor_scalar(
                 out=minus[:],
                 in0=maxes[g][:, 0:1],
@@ -192,12 +190,12 @@ def tile_visionattention_pa_kernel(tc, x, Wq, bq, k, out):
             neg_max[g] = minus
 
         def exponentials(g):
-            row_tile = row_pool.tile([P, TOKENS], F32, tag="probs")
-            bank_sums = row_pool.tile([P, HALVES], F32, tag="sums")
+            row_tile = rows_pool.tile([P, TOKENS], F32, tag="probs")
+            bank_sums = rows_pool.tile([P, HALVES], F32, tag="sums")
             for h in range(HALVES):
                 nc.scalar.activation(
-                    out=row_tile[:, h * HALF : (h + 1) * HALF],
-                    in_=scores[g][h][:],
+                    out=row_tile[:, h * HALF : (h + 1) * HALF].rearrange("p (r a) -> p r a", a=PACK),
+                    in_=scores[g][h][:].rearrange("p (a r) -> p r a", a=PACK),
                     func=ACT.Exp,
                     bias=neg_max[g][:, 0:1],
                     scale=1.0,
@@ -207,61 +205,54 @@ def tile_visionattention_pa_kernel(tc, x, Wq, bq, k, out):
             sums[g] = bank_sums
 
         def add_sums(g):
-            total = row_pool.tile([P, 1], F32, tag="row_sum")
+            total = rows_pool.tile([P, 1], F32, tag="row_sum")
             nc.vector.tensor_add(out=total[:], in0=sums[g][:, 0:1], in1=sums[g][:, 1:2])
             row_sum[g] = total
 
         def invert_sum(g):
-            inverse = row_pool.tile([P, 1], F32, tag="inv_sum")
+            inverse = rows_pool.tile([P, 1], F32, tag="inv_sum")
             nc.vector.reciprocal(out=inverse[:], in_=row_sum[g][:])
             inv_sum[g] = inverse
 
         def scale_and_store(g):
-            nc.gpsimd.tensor_scalar(
-                out=probs[g][:],
-                in0=probs[g][:],
-                scalar1=inv_sum[g][:, 0:1],
-                scalar2=0.0,
-                op0=ALU.mult,
-                op1=ALU.add,
-            )
-            nc.sync.dma_start(out=out_rows_dram[g * P : (g + 1) * P, :], in_=probs[g][:])
+            rows = slice(g * P, (g + 1) * P)
+            if g < TILES - LAG:
+                nc.gpsimd.tensor_scalar(
+                    out=probs[g][:],
+                    in0=probs[g][:],
+                    scalar1=inv_sum[g][:, 0:1],
+                    scalar2=0.0,
+                    op0=ALU.mult,
+                    op1=ALU.add,
+                )
+                nc.sync.dma_start(out=out_rows_dram[rows, :], in_=probs[g][:])
+            else:
+                for h in range(HALVES):
+                    cols = slice(h * HALF, (h + 1) * HALF)
+                    nc.vector.tensor_scalar_mul(
+                        out=probs[g][:, cols], in0=probs[g][:, cols], scalar1=inv_sum[g][:, 0:1]
+                    )
+                    nc.sync.dma_start(out=out_rows_dram[rows, cols], in_=probs[g][:, cols])
 
         def is_tile(g):
             return 0 <= g < TILES
 
-        def step(s):
-            if is_tile(s + LEAD):
-                project(s + LEAD)
-            if s >= 0 and is_tile(s + 1):
-                score(s + 1)
-            if is_tile(s + LEAD):
-                leave_psum(s + LEAD)
-            if is_tile(s):
-                bank_maximum(s, 0)
-            if is_tile(s - LAG):
-                add_sums(s - LAG)
-            if is_tile(s):
-                bank_maximum(s, 1)
-            if is_tile(s + PACK_LEAD):
-                pack(s + PACK_LEAD)
-            if is_tile(s - LAG):
-                invert_sum(s - LAG)
-            if is_tile(s):
-                negate_maximum(s)
-                exponentials(s)
-            if is_tile(s - LAG):
-                scale_and_store(s - LAG)
-
-        k_grouped = []
-        k_grouped.append(channels_to_partitions(nc, keep, banks, identity, k_rows[0], "k0"))
-        step(-LEAD)
-        step(-LEAD + 1)
-        k_grouped.append(channels_to_partitions(nc, keep, banks, identity, k_rows[1], "k1"))
-        for s in range(-LEAD + 2, 0):
-            step(s)
-        for h in range(HALVES):
-            k_mx.append(quantise(nc, keep, k_grouped[h], "k%d" % h))
-        score(0)
-        for s in range(0, TILES + LAG):
-            step(s)
+        with tc.manual_schedule():
+            for g in range(SCORE_LEAD):
+                score(g)
+            for s in range(TILES + LAG):
+                if is_tile(s + SCORE_LEAD):
+                    score(s + SCORE_LEAD)
+                if is_tile(s):
+                    bank_maximum(s, 0)
+                if is_tile(s - LAG):
+                    add_sums(s - LAG)
+                if is_tile(s):
+                    bank_maximum(s, 1)
+                if is_tile(s - LAG):
+                    invert_sum(s - LAG)
+                if is_tile(s):
+                    negate_maximum(s)
+                    exponentials(s)
+                if is_tile(s - LAG):
+                    scale_and_store(s - LAG)

import math
from contextlib import ExitStack

import concourse.masks as masks
import concourse.mybir as mybir

F32 = mybir.dt.float32
BF16 = mybir.dt.bfloat16
U32 = mybir.dt.uint32
U8 = mybir.dt.uint8
FP8X4 = mybir.dt.float8_e4m3fn_x4
ACT = mybir.ActivationFunctionType
ALU = mybir.AluOpType
AXIS = mybir.AxisListType

P = 128
PACK = 4
CHANNELS = P * PACK
TOKENS = 1024
HALF = 512
HALVES = TOKENS // HALF
WORD_PAIR = 2
INV_SQRT_CHANNELS = 1.0 / math.sqrt(CHANNELS)
TILES = TOKENS // P
SCORE_LEAD = 2
LAG = 2

FLOPS = 2 * TOKENS * CHANNELS * CHANNELS + 2 * TOKENS * TOKENS * CHANNELS


def quantise(nc, pool, grouped, label):
    codes = pool.tile([P, HALF], U32, name="%s_codes" % label, align_bytes=64)
    scales = pool.tile([P, HALF], U8, name="%s_scales" % label, align_bytes=64)
    nc.vector.quantize_mx(out=codes[:].bitcast(FP8X4), scales=scales[:], in_=grouped[:])
    return codes, scales


def interleave_planes(nc, pool, planes, label):
    grouped = pool.tile([P, HALF * PACK], BF16, name="%s_grouped" % label, align_bytes=64)
    nc.vector.tensor_copy(
        out=grouped[:].rearrange("p (c i t) -> p c t i", i=4, t=PACK),
        in_=planes[:].rearrange("p t (c i) -> p c t i", i=4),
    )
    return grouped


def channels_to_partitions(nc, pool, psum, identity, rows, label):
    row_words = rows[:].bitcast(F32).rearrange("p (a u w) -> p a u w", a=PACK, u=WORD_PAIR)
    grouped = pool.tile([P, HALF * PACK], BF16, name="%s_grouped" % label, align_bytes=64)
    grouped_words = grouped[:].bitcast(F32).rearrange("p (a r u) -> p a r u", a=PACK, u=WORD_PAIR)
    tiles_per_bank = 2
    for first in range(0, PACK, tiles_per_bank):
        bank = psum.tile([P, HALF], F32, tag="bank")
        flipped = bank[:].rearrange("p (a u r) -> p a u r", a=tiles_per_bank, u=WORD_PAIR)
        for a in range(tiles_per_bank):
            for u in range(WORD_PAIR):
                nc.tensor.transpose(flipped[:, a, u, :], row_words[:, first + a, u, :], identity[:])
        nc.scalar.copy(
            out=grouped_words[:, first : first + tiles_per_bank],
            in_=flipped.rearrange("p a u r -> p a r u"),
        )
    return grouped


def tile_visionattention_pa_kernel(tc, x, Wq, bq, k, out):
    nc = tc.nc
    x_rows_dram = x.rearrange("b c h w -> (b c) (h w)")
    k_rows_dram = k.flatten_outer_dims()
    out_rows_dram = out.flatten_outer_dims()

    with ExitStack() as ctx:
        keep = ctx.enter_context(tc.tile_pool(name="keep", bufs=1))
        rows_pool = ctx.enter_context(tc.tile_pool(name="rows", bufs=LAG + 3))
        psum = ctx.enter_context(tc.psum_pool(name="psum", bufs=8))

        wq_rows = keep.tile([P, PACK * CHANNELS], BF16)
        nc.sync.dma_start(
            out=wq_rows[:].rearrange("r (u ec) -> r u ec", u=WORD_PAIR),
            in_=Wq.rearrange("(u r e) c -> r u (e c)", u=WORD_PAIR, e=2),
        )
        x_planes = []
        k_rows = []
        for h in range(HALVES):
            cols = slice(h * HALF, (h + 1) * HALF)
            x_half = keep.tile([P, PACK, HALF], BF16, name="x_planes%d" % h)
            for u in range(WORD_PAIR):
                nc.sync.dma_start(
                    out=x_half[:, 2 * u : 2 * u + 2, :],
                    in_=x_rows_dram[u * 2 * P : (u + 1) * 2 * P, cols].rearrange("(p e) n -> p e n", e=2),
                )
            x_planes.append(x_half)
            k_half = keep.tile([P, PACK * CHANNELS], BF16, name="k_rows%d" % h)
            nc.sync.dma_start(out=k_half[:], in_=k_rows_dram[cols, :].rearrange("(r a) c -> r (a c)", a=PACK))
            k_rows.append(k_half)
        bq_raw = keep.tile([P, PACK], BF16)
        nc.scalar.dma_start(
            out=bq_raw[:].rearrange("r (u e) -> r u e", u=WORD_PAIR),
            in_=bq.rearrange("(u r e) -> r u e", u=WORD_PAIR, e=2),
        )

        identity = keep.tile([P, P], F32)
        masks.make_identity(nc, identity[:])
        warm = keep.tile([P, 1], F32)
        nc.vector.memset(warm[:], 0.0)
        nc.scalar.activation(out=warm[:], in_=warm[:], func=ACT.Exp)
        bias = keep.tile([P, PACK], F32)
        nc.vector.tensor_scalar_mul(out=bias[:], in0=bq_raw[:], scalar1=INV_SQRT_CHANNELS)

        wq_grouped = channels_to_partitions(nc, keep, psum, identity, wq_rows, "wq")
        wq_codes, wq_scales = quantise(nc, keep, wq_grouped, "wq")

        x_mx = []
        k_mx = []
        for h in range(HALVES):
            x_grouped = interleave_planes(nc, keep, x_planes[h], "x%d" % h)
            x_mx.append(quantise(nc, keep, x_grouped, "x%d" % h))
            k_grouped = channels_to_partitions(nc, keep, psum, identity, k_rows[h], "k%d" % h)
            k_mx.append(quantise(nc, keep, k_grouped, "k%d" % h))

        q_mx = []
        for h in range(HALVES):
            x_codes, x_scales = x_mx[h]
            q_planes = keep.tile([P, PACK, HALF], BF16, name="q_planes%d" % h)
            for t in range(PACK):
                out_channels = slice(t * P, (t + 1) * P)
                bank = psum.tile([P, HALF], F32, tag="bank")
                nc.tensor.matmul_mx(
                    out=bank[:],
                    lhsT=wq_codes[:, out_channels].bitcast(FP8X4),
                    lhsT_scale=wq_scales[:, out_channels],
                    rhs=x_codes[:].bitcast(FP8X4),
                    rhs_scale=x_scales[:],
                    start=True,
                    stop=True,
                )
                nc.scalar.activation(
                    out=q_planes[:, t, :],
                    in_=bank[:],
                    func=ACT.Identity,
                    bias=bias[:, t : t + 1],
                    scale=INV_SQRT_CHANNELS,
                )
            q_grouped = interleave_planes(nc, keep, q_planes, "q%d" % h)
            q_mx.append(quantise(nc, keep, q_grouped, "q%d" % h))

        scores = {}
        maxes = {}
        neg_max = {}
        probs = {}
        sums = {}
        row_sum = {}
        inv_sum = {}

        def score(g):
            q_codes, q_scales = q_mx[(g * P) // HALF]
            tokens = slice((g * P) % HALF, (g * P) % HALF + P)
            scores[g] = []
            for h in range(HALVES):
                k_codes, k_scales = k_mx[h]
                bank = psum.tile([P, HALF], F32, tag="bank")
                nc.tensor.matmul_mx(
                    out=bank[:],
                    lhsT=q_codes[:, tokens].bitcast(FP8X4),
                    lhsT_scale=q_scales[:, tokens],
                    rhs=k_codes[:].bitcast(FP8X4),
                    rhs_scale=k_scales[:],
                    start=True,
                    stop=True,
                )
                scores[g].append(bank)

        def bank_maximum(g, h):
            if h == 0:
                bank_maxes = rows_pool.tile([P, HALVES], F32, tag="maxes")
                maxes[g] = bank_maxes
            nc.vector.tensor_reduce(
                out=maxes[g][:, h : h + 1], in_=scores[g][h][:], axis=AXIS.X, op=ALU.max
            )

        def negate_maximum(g):
            minus = rows_pool.tile([P, 1], F32, tag="neg_max")
            nc.vector.tensor_scalar(
                out=minus[:],
                in0=maxes[g][:, 0:1],
                scalar1=maxes[g][:, 1:2],
                scalar2=-1.0,
                op0=ALU.max,
                op1=ALU.mult,
            )
            neg_max[g] = minus

        def exponentials(g):
            row_tile = rows_pool.tile([P, TOKENS], F32, tag="probs")
            bank_sums = rows_pool.tile([P, HALVES], F32, tag="sums")
            for h in range(HALVES):
                nc.scalar.activation(
                    out=row_tile[:, h * HALF : (h + 1) * HALF].rearrange("p (r a) -> p r a", a=PACK),
                    in_=scores[g][h][:].rearrange("p (a r) -> p r a", a=PACK),
                    func=ACT.Exp,
                    bias=neg_max[g][:, 0:1],
                    scale=1.0,
                    accum_out=bank_sums[:, h : h + 1],
                )
            probs[g] = row_tile
            sums[g] = bank_sums

        def add_sums(g):
            total = rows_pool.tile([P, 1], F32, tag="row_sum")
            nc.vector.tensor_add(out=total[:], in0=sums[g][:, 0:1], in1=sums[g][:, 1:2])
            row_sum[g] = total

        def invert_sum(g):
            inverse = rows_pool.tile([P, 1], F32, tag="inv_sum")
            nc.vector.reciprocal(out=inverse[:], in_=row_sum[g][:])
            inv_sum[g] = inverse

        def scale_and_store(g):
            rows = slice(g * P, (g + 1) * P)
            if g < TILES - LAG:
                nc.gpsimd.tensor_scalar(
                    out=probs[g][:],
                    in0=probs[g][:],
                    scalar1=inv_sum[g][:, 0:1],
                    scalar2=0.0,
                    op0=ALU.mult,
                    op1=ALU.add,
                )
                nc.sync.dma_start(out=out_rows_dram[rows, :], in_=probs[g][:])
            else:
                for h in range(HALVES):
                    cols = slice(h * HALF, (h + 1) * HALF)
                    nc.vector.tensor_scalar_mul(
                        out=probs[g][:, cols], in0=probs[g][:, cols], scalar1=inv_sum[g][:, 0:1]
                    )
                    nc.sync.dma_start(out=out_rows_dram[rows, cols], in_=probs[g][:, cols])

        def is_tile(g):
            return 0 <= g < TILES

        with tc.manual_schedule():
            for g in range(SCORE_LEAD):
                score(g)
            for s in range(TILES + LAG):
                if is_tile(s + SCORE_LEAD):
                    score(s + SCORE_LEAD)
                if is_tile(s):
                    bank_maximum(s, 0)
                if is_tile(s - LAG):
                    add_sums(s - LAG)
                if is_tile(s):
                    bank_maximum(s, 1)
                if is_tile(s - LAG):
                    invert_sum(s - LAG)
                if is_tile(s):
                    negate_maximum(s)
                    exponentials(s)
                if is_tile(s - LAG):
                    scale_and_store(s - LAG)
